import numpy as np
import ml_dtypes


def mxq(x, axis, fmt="e4m3"):
    dtype, down = {"e4m3": (ml_dtypes.float8_e4m3fn, 7), "e5m2": (ml_dtypes.float8_e5m2, 14)}[fmt]
    v = np.moveaxis(np.asarray(x, np.float32).astype(ml_dtypes.bfloat16).astype(np.float64), axis, -1)
    blocks = v.reshape(v.shape[:-1] + (-1, 32))
    amax = np.abs(blocks).max(-1, keepdims=True)
    byte = np.maximum(np.where(amax > 0, np.frexp(amax)[1] - 1 + 127, 0) - down, 1)
    scale = np.exp2(byte - 127.0)
    codes = (blocks / scale).astype(np.float32).astype(dtype).astype(np.float64)
    return np.moveaxis((codes * scale).reshape(v.shape), -1, axis)


WIDE = False


def mx_kscale(k):
    if not WIDE:
        return np.ones(k)
    levels = np.array([10, -10, 5, -5, 0])
    a = np.random.permutation(np.resize(levels, k // 512 * 4)).reshape(k // 512, 4)
    idx = np.arange(k)
    return np.exp2(a[idx // 512, idx % 128 // 32])


BF16 = ml_dtypes.bfloat16


def bf(x):
    return np.asarray(x, np.float32).astype(BF16)


def f64(x):
    return np.asarray(x).astype(np.float64)


H, N, S, T, L, K = 2, 2, 128, 512, 1024, 512
NH = N * H


def rel_shift(p):
    zero_pad = np.zeros((NH, S, 1))
    padded = np.concatenate([zero_pad, p], axis=2)
    padded = padded.reshape(NH, T + 1, S)
    return padded[:, 1:, :].reshape(NH, S, T)


def setup_inputs():
    s = mx_kscale(K)
    return {"queries": bf(np.random.standard_normal((NH, S, K)) * s),
            "v_bias": bf(np.random.standard_normal((1, H, 1, K)) / np.sqrt(K) * s),
            "R": bf(np.random.standard_normal((H, L, K)) / s)}


def reference(queries, v_bias, R):
    q = (f64(queries) * K ** -0.5).reshape(N, H, S, K)
    q_v = q + f64(v_bias)
    r = f64(R)[:, :T, :]
    pos = mxq(q_v, 3, "e4m3") @ mxq(r, 2, "e4m3").transpose(0, 2, 1)
    return rel_shift(pos.reshape(NH, S, T))

@@ -1,0 +1,150 @@
+import concourse.mybir as mybir
+from concourse.masks import make_identity
+
+F32 = mybir.dt.float32
+BF16 = mybir.dt.bfloat16
+U32 = mybir.dt.uint32
+U8 = mybir.dt.uint8
+FP8X4 = mybir.dt.float8_e4m3fn_x4
+MULT = mybir.AluOpType.mult
+ADD = mybir.AluOpType.add
+
+P = 128
+SEQS = 2
+HEADS = 2
+S = 128
+T = 512
+K = 512
+PACK = 4
+HALVES = 2
+T_CHUNK = 256
+CHUNKS = T // T_CHUNK
+ROW_TILES = T_CHUNK // P
+PADDED = T + 1
+PADDED_PITCH = 520
+DROPPED = S
+SMALL_ROWS = 16
+
+FLOPS = 2 * SEQS * HEADS * S * T * K
+BYTES = 2 * (SEQS * HEADS * S * K + HEADS * K + HEADS * T * K) + 4 * SEQS * HEADS * S * T
+
+
+def tile_relativepositionsdpa_pa_s_kernel(tc, queries, v_bias, R, out):
+    nc = tc.nc
+    with tc.tile_pool(name="keep", bufs=1) as keep, tc.psum_pool(
+        name="transposed", bufs=4
+    ) as transposed, tc.psum_pool(name="scores", bufs=4) as scores:
+        bias_rows = keep.tile([P, K // HALVES], BF16, name="bias_rows")
+        nc.vector.memset(bias_rows[:], 0.0)
+        nc.scalar.dma_start(
+            out=bias_rows[0 : HEADS * HALVES, :],
+            in_=v_bias.rearrange("o h i (u w) -> (o h i u) w", u=HALVES),
+        )
+        q_by_head = queries.rearrange("(n h) s k -> h s n k", h=HEADS)
+        q_raw = []
+        r_raw = []
+        for h in range(HEADS):
+            q_tile = keep.tile([P, SEQS, K], BF16, name="q_raw%d" % h)
+            nc.sync.dma_start(out=q_tile[:], in_=q_by_head[h])
+            q_raw.append(q_tile)
+            for c in range(CHUNKS):
+                r_tile = keep.tile([P, ROW_TILES, K], BF16, name="r_raw%d_%d" % (h, c))
+                nc.sync.dma_start(
+                    out=r_tile[:],
+                    in_=R[h, c * T_CHUNK : (c + 1) * T_CHUNK, :].rearrange("(a r) k -> r a k", a=ROW_TILES),
+                )
+                r_raw.append(r_tile)
+
+        identity = keep.tile([P, P], F32, name="identity")
+        make_identity(nc, identity[:])
+
+        padded = []
+        for h in range(HEADS):
+            padded_tile = keep.tile([P, SEQS, PADDED_PITCH], F32, name="padded%d" % h)
+            nc.gpsimd.memset(padded_tile[:, :, 0:8], 0.0)
+            padded.append(padded_tile)
+
+        q_codes = keep.tile([P, HEADS, SEQS * S], U32, name="q_codes", align_bytes=64)
+        q_scales = keep.tile([P, HEADS, SEQS * S], U8, name="q_scales", align_bytes=64)
+        r_codes = keep.tile([P, HEADS, T], U32, name="r_codes", align_bytes=64)
+        r_scales = keep.tile([P, HEADS, T], U8, name="r_scales", align_bytes=64)
+
+        bias_t = transposed.tile([P, P], F32, tag="t", name="bias_t")
+        nc.tensor.transpose(bias_t[:], bias_rows[:].bitcast(F32), identity[:])
+        bias_words = keep.tile([P, HEADS * HALVES], F32, name="bias_words")
+        nc.vector.tensor_copy(out=bias_words[:], in_=bias_t[:, 0 : HEADS * HALVES])
+        bias_values = bias_words[:].bitcast(BF16)
+
+        out_by_head = out.rearrange("(n h) s t -> h n (s t)", h=HEADS)
+
+        for h in range(HEADS):
+            q_words = q_raw[h][:].bitcast(F32)
+            q_t = transposed.tile([P, HALVES, SEQS, S], F32, tag="t", name="q_t%d" % h)
+            for u in range(HALVES):
+                for n in range(SEQS):
+                    nc.tensor.transpose(q_t[:, u, n, :], q_words[:, n, u * P : (u + 1) * P], identity[:])
+            q_grouped = keep.tile([P, SEQS * S, PACK], BF16, name="q_grouped%d" % h, align_bytes=64)
+            for u in range(HALVES):
+                first = h * PACK + u * 2
+                nc.vector.scalar_tensor_tensor(
+                    out=q_grouped[:, :, u * 2 : u * 2 + 2],
+                    in0=q_t[:, u, :, :].rearrange("p n s -> p (n s)").bitcast(BF16).rearrange("p (g e) -> p g e", e=2),
+                    scalar=K**-0.5,
+                    in1=bias_values[:, first : first + 2].unsqueeze(1).to_broadcast([P, SEQS * S, 2]),
+                    op0=MULT,
+                    op1=ADD,
+                )
+            nc.vector.quantize_mx(
+                out=q_codes[:, h, :].bitcast(FP8X4),
+                scales=q_scales[:, h, :],
+                in_=q_grouped[:].rearrange("p g t -> p (g t)"),
+            )
+
+            for c in range(CHUNKS):
+                cols = slice(c * T_CHUNK, (c + 1) * T_CHUNK)
+                r_words = r_raw[h * CHUNKS + c][:].bitcast(F32)
+                r_t = transposed.tile([P, ROW_TILES, HALVES, P], F32, tag="t", name="r_t%d_%d" % (h, c))
+                for a in range(ROW_TILES):
+                    for u in range(HALVES):
+                        nc.tensor.transpose(r_t[:, a, u, :], r_words[:, a, u * P : (u + 1) * P], identity[:])
+                r_grouped = keep.tile([P, T_CHUNK * PACK], BF16, name="r_grouped%d_%d" % (h, c), align_bytes=64)
+                nc.scalar.copy(
+                    out=r_grouped[:].bitcast(F32).rearrange("p (a r u) -> p a r u", a=ROW_TILES, u=HALVES),
+                    in_=r_t[:].rearrange("p a u r -> p a r u"),
+                )
+                nc.vector.quantize_mx(
+                    out=r_codes[:, h, cols].bitcast(FP8X4),
+                    scales=r_scales[:, h, cols],
+                    in_=r_grouped[:],
+                )
+                for n in range(SEQS):
+                    pos = scores.tile([P, T_CHUNK], F32, tag="pos", name="pos%d_%d_%d" % (h, c, n))
+                    nc.tensor.matmul_mx(
+                        out=pos[:],
+                        lhsT=q_codes[:, h, n * S : (n + 1) * S].bitcast(FP8X4),
+                        lhsT_scale=q_scales[:, h, n * S : (n + 1) * S],
+                        rhs=r_codes[:, h, cols].bitcast(FP8X4),
+                        rhs_scale=r_scales[:, h, cols],
+                        start=True,
+                        stop=True,
+                    )
+                    target = padded[h][:, n, 1 + c * T_CHUNK : 1 + (c + 1) * T_CHUNK]
+                    if n == 0:
+                        nc.vector.tensor_copy(out=target, in_=pos[:])
+                    else:
+                        nc.scalar.copy(out=target, in_=pos[:])
+
+            flat = out_by_head[h]
+            split = SMALL_ROWS * PADDED - DROPPED
+            nc.sync.dma_start(
+                out=flat[:, split:].rearrange("n (s c) -> s n c", c=PADDED),
+                in_=padded[h][SMALL_ROWS:P, :, 0:PADDED],
+            )
+            nc.sync.dma_start(
+                out=flat[:, PADDED - DROPPED : split].rearrange("n (s c) -> s n c", c=PADDED),
+                in_=padded[h][1:SMALL_ROWS, :, 0:PADDED],
+            )
+            nc.sync.dma_start(
+                out=flat[:, 0 : PADDED - DROPPED].unsqueeze(0),
+                in_=padded[h][0:1, :, DROPPED:PADDED],
+            )

@@ -12,6 +12,7 @@ ADD = mybir.AluOpType.add
 P = 128
 SEQS = 2
 HEADS = 2
+BATCHES = SEQS * HEADS
 S = 128
 T = 512
 K = 512
@@ -19,14 +20,15 @@ PACK = 4
 HALVES = 2
 T_CHUNK = 256
 CHUNKS = T // T_CHUNK
-ROW_TILES = T_CHUNK // P
+ROWS_EACH = T_CHUNK // P
 PADDED = T + 1
-PADDED_PITCH = 520
+LEAD = 7
+PITCH = LEAD + PADDED
 DROPPED = S
 SMALL_ROWS = 16
 
-FLOPS = 2 * SEQS * HEADS * S * T * K
-BYTES = 2 * (SEQS * HEADS * S * K + HEADS * K + HEADS * T * K) + 4 * SEQS * HEADS * S * T
+FLOPS = 2 * BATCHES * S * T * K
+BYTES = 2 * (BATCHES * S * K + HEADS * K + HEADS * T * K) + 4 * BATCHES * S * T
 
 
 def tile_relativepositionsdpa_pa_s_kernel(tc, queries, v_bias, R, out):
@@ -40,32 +42,28 @@ def tile_relativepositionsdpa_pa_s_kernel(tc, queries, v_bias, R, out):
             out=bias_rows[0 : HEADS * HALVES, :],
             in_=v_bias.rearrange("o h i (u w) -> (o h i u) w", u=HALVES),
         )
-        q_by_head = queries.rearrange("(n h) s k -> h s n k", h=HEADS)
-        q_raw = []
-        r_raw = []
+        q_raw = keep.tile([P, BATCHES, K], BF16, name="q_raw")
+        r_raw = keep.tile([P, HEADS, CHUNKS, ROWS_EACH * K], BF16, name="r_raw")
         for h in range(HEADS):
-            q_tile = keep.tile([P, SEQS, K], BF16, name="q_raw%d" % h)
-            nc.sync.dma_start(out=q_tile[:], in_=q_by_head[h])
-            q_raw.append(q_tile)
             for c in range(CHUNKS):
-                r_tile = keep.tile([P, ROW_TILES, K], BF16, name="r_raw%d_%d" % (h, c))
                 nc.sync.dma_start(
-                    out=r_tile[:],
-                    in_=R[h, c * T_CHUNK : (c + 1) * T_CHUNK, :].rearrange("(a r) k -> r a k", a=ROW_TILES),
+                    out=r_raw[:, h, c, :],
+                    in_=R[h, c * T_CHUNK : (c + 1) * T_CHUNK, :].rearrange("(r a) k -> r (a k)", a=ROWS_EACH),
                 )
-                r_raw.append(r_tile)
+            for n in range(SEQS):
+                b = n * HEADS + h
+                nc.sync.dma_start(out=q_raw[:, b, :], in_=queries[b])
 
         identity = keep.tile([P, P], F32, name="identity")
         make_identity(nc, identity[:])
 
-        padded = []
-        for h in range(HEADS):
-            padded_tile = keep.tile([P, SEQS, PADDED_PITCH], F32, name="padded%d" % h)
-            nc.gpsimd.memset(padded_tile[:, :, 0:8], 0.0)
-            padded.append(padded_tile)
+        padded = keep.tile([P, BATCHES, PITCH], F32, name="padded")
+        nc.gpsimd.memset(padded[:, :, 0 : LEAD + 1], 0.0)
 
-        q_codes = keep.tile([P, HEADS, SEQS * S], U32, name="q_codes", align_bytes=64)
-        q_scales = keep.tile([P, HEADS, SEQS * S], U8, name="q_scales", align_bytes=64)
+        q_grouped = keep.tile([P, BATCHES, S * PACK], BF16, name="q_grouped", align_bytes=64)
+        r_grouped = keep.tile([P, HEADS, T * PACK], BF16, name="r_grouped", align_bytes=64)
+        q_codes = keep.tile([P, BATCHES, S], U32, name="q_codes", align_bytes=64)
+        q_scales = keep.tile([P, BATCHES, S], U8, name="q_scales", align_bytes=64)
         r_codes = keep.tile([P, HEADS, T], U32, name="r_codes", align_bytes=64)
         r_scales = keep.tile([P, HEADS, T], U8, name="r_scales", align_bytes=64)
 
@@ -75,76 +73,71 @@ def tile_relativepositionsdpa_pa_s_kernel(tc, queries, v_bias, R, out):
         nc.vector.tensor_copy(out=bias_words[:], in_=bias_t[:, 0 : HEADS * HALVES])
         bias_values = bias_words[:].bitcast(BF16)
 
-        out_by_head = out.rearrange("(n h) s t -> h n (s t)", h=HEADS)
-
         for h in range(HEADS):
-            q_words = q_raw[h][:].bitcast(F32)
-            q_t = transposed.tile([P, HALVES, SEQS, S], F32, tag="t", name="q_t%d" % h)
-            for u in range(HALVES):
-                for n in range(SEQS):
-                    nc.tensor.transpose(q_t[:, u, n, :], q_words[:, n, u * P : (u + 1) * P], identity[:])
-            q_grouped = keep.tile([P, SEQS * S, PACK], BF16, name="q_grouped%d" % h, align_bytes=64)
-            for u in range(HALVES):
-                first = h * PACK + u * 2
+            for c in range(CHUNKS):
+                r_words = r_raw[:, h, c, :].bitcast(F32).rearrange("p (a u w) -> p a u w", a=ROWS_EACH, u=HALVES)
+                r_t = transposed.tile([P, ROWS_EACH, HALVES, P], F32, tag="t", name="r_t%d_%d" % (h, c))
+                for a in range(ROWS_EACH):
+                    for u in range(HALVES):
+                        nc.tensor.transpose(r_t[:, a, u, :], r_words[:, a, u, :], identity[:])
+                piece = r_grouped[:, h, c * T_CHUNK * PACK : (c + 1) * T_CHUNK * PACK]
+                nc.scalar.copy(
+                    out=piece.bitcast(F32).rearrange("p (r a u) -> p r a u", a=ROWS_EACH, u=HALVES),
+                    in_=r_t[:].rearrange("p a u r -> p r a u"),
+                )
+                cols = slice(c * T_CHUNK, (c + 1) * T_CHUNK)
+                nc.vector.quantize_mx(
+                    out=r_codes[:, h, cols].bitcast(FP8X4), scales=r_scales[:, h, cols], in_=piece
+                )
+            for n in range(SEQS):
+                b = n * HEADS + h
+                q_words = q_raw[:, b, :].bitcast(F32)
+                q_t = transposed.tile([P, S, HALVES], F32, tag="t", name="q_t%d" % b)
+                for u in range(HALVES):
+                    nc.tensor.transpose(q_t[:, :, u], q_words[:, u * P : (u + 1) * P], identity[:])
                 nc.vector.scalar_tensor_tensor(
-                    out=q_grouped[:, :, u * 2 : u * 2 + 2],
-                    in0=q_t[:, u, :, :].rearrange("p n s -> p (n s)").bitcast(BF16).rearrange("p (g e) -> p g e", e=2),
+                    out=q_grouped[:, b, :].rearrange("p (s t) -> p s t", t=PACK),
+                    in0=q_t[:].rearrange("p s u -> p (s u)").bitcast(BF16).rearrange("p (s t) -> p s t", t=PACK),
                     scalar=K**-0.5,
-                    in1=bias_values[:, first : first + 2].unsqueeze(1).to_broadcast([P, SEQS * S, 2]),
+                    in1=bias_values[:, h * PACK : (h + 1) * PACK].unsqueeze(1).to_broadcast([P, S, PACK]),
                     op0=MULT,
                     op1=ADD,
                 )
-            nc.vector.quantize_mx(
-                out=q_codes[:, h, :].bitcast(FP8X4),
-                scales=q_scales[:, h, :],
-                in_=q_grouped[:].rearrange("p g t -> p (g t)"),
-            )
-
-            for c in range(CHUNKS):
-                cols = slice(c * T_CHUNK, (c + 1) * T_CHUNK)
-                r_words = r_raw[h * CHUNKS + c][:].bitcast(F32)
-                r_t = transposed.tile([P, ROW_TILES, HALVES, P], F32, tag="t", name="r_t%d_%d" % (h, c))
-                for a in range(ROW_TILES):
-                    for u in range(HALVES):
-                        nc.tensor.transpose(r_t[:, a, u, :], r_words[:, a, u * P : (u + 1) * P], identity[:])
-                r_grouped = keep.tile([P, T_CHUNK * PACK], BF16, name="r_grouped%d_%d" % (h, c), align_bytes=64)
-                nc.scalar.copy(
-                    out=r_grouped[:].bitcast(F32).rearrange("p (a r u) -> p a r u", a=ROW_TILES, u=HALVES),
-                    in_=r_t[:].rearrange("p a u r -> p a r u"),
-                )
                 nc.vector.quantize_mx(
-                    out=r_codes[:, h, cols].bitcast(FP8X4),
-                    scales=r_scales[:, h, cols],
-                    in_=r_grouped[:],
+                    out=q_codes[:, b, :].bitcast(FP8X4), scales=q_scales[:, b, :], in_=q_grouped[:, b, :]
                 )
-                for n in range(SEQS):
-                    pos = scores.tile([P, T_CHUNK], F32, tag="pos", name="pos%d_%d_%d" % (h, c, n))
+
+        for h in range(HEADS):
+            for n in range(SEQS):
+                b = n * HEADS + h
+                for c in range(CHUNKS):
+                    cols = slice(c * T_CHUNK, (c + 1) * T_CHUNK)
+                    pos = scores.tile([P, T_CHUNK], F32, tag="pos", name="pos%d_%d" % (b, c))
                     nc.tensor.matmul_mx(
                         out=pos[:],
-                        lhsT=q_codes[:, h, n * S : (n + 1) * S].bitcast(FP8X4),
-                        lhsT_scale=q_scales[:, h, n * S : (n + 1) * S],
+                        lhsT=q_codes[:, b, :].bitcast(FP8X4),
+                        lhsT_scale=q_scales[:, b, :],
                         rhs=r_codes[:, h, cols].bitcast(FP8X4),
                         rhs_scale=r_scales[:, h, cols],
                         start=True,
                         stop=True,
                     )
-                    target = padded[h][:, n, 1 + c * T_CHUNK : 1 + (c + 1) * T_CHUNK]
-                    if n == 0:
-                        nc.vector.tensor_copy(out=target, in_=pos[:])
+                    first = LEAD + 1 + c * T_CHUNK
+                    if c == 0:
+                        nc.vector.tensor_copy(out=padded[:, b, first : first + T_CHUNK], in_=pos[:])
                     else:
-                        nc.scalar.copy(out=target, in_=pos[:])
-
-            flat = out_by_head[h]
-            split = SMALL_ROWS * PADDED - DROPPED
-            nc.sync.dma_start(
-                out=flat[:, split:].rearrange("n (s c) -> s n c", c=PADDED),
-                in_=padded[h][SMALL_ROWS:P, :, 0:PADDED],
-            )
-            nc.sync.dma_start(
-                out=flat[:, PADDED - DROPPED : split].rearrange("n (s c) -> s n c", c=PADDED),
-                in_=padded[h][1:SMALL_ROWS, :, 0:PADDED],
-            )
-            nc.sync.dma_start(
-                out=flat[:, 0 : PADDED - DROPPED].unsqueeze(0),
-                in_=padded[h][0:1, :, DROPPED:PADDED],
-            )
+                        nc.scalar.copy(out=padded[:, b, first : first + T_CHUNK], in_=pos[:])
+                flat = out[b].rearrange("s t -> (s t)")
+                split = SMALL_ROWS * PADDED - DROPPED
+                nc.sync.dma_start(
+                    out=flat[split:].rearrange("(s c) -> s c", c=PADDED),
+                    in_=padded[SMALL_ROWS:P, b, LEAD:PITCH],
+                )
+                nc.sync.dma_start(
+                    out=flat[PADDED - DROPPED : split].rearrange("(s c) -> s c", c=PADDED),
+                    in_=padded[1:SMALL_ROWS, b, LEAD:PITCH],
+                )
+                nc.sync.dma_start(
+                    out=flat[0 : PADDED - DROPPED].unsqueeze(0),
+                    in_=padded[0:1, b, LEAD + DROPPED : PITCH],
+                )

@@ -22,48 +22,57 @@ T_CHUNK = 256
 CHUNKS = T // T_CHUNK
 ROWS_EACH = T_CHUNK // P
 PADDED = T + 1
-LEAD = 7
-PITCH = LEAD + PADDED
 DROPPED = S
-SMALL_ROWS = 16
+BLOCK = 8
+LEAD = BLOCK - 1
+PITCH = LEAD + PADDED
+GROUP = BLOCK * PADDED
+GROUPS = S // BLOCK
+LEAD_COLS = 128
 
 FLOPS = 2 * BATCHES * S * T * K
 BYTES = 2 * (BATCHES * S * K + HEADS * K + HEADS * T * K) + 4 * BATCHES * S * T
 
 
+def runs_a_group_apart(flat, first, count, length):
+    slack = min(first, GROUP - length)
+    window = flat[:, first - slack : first - slack + count * GROUP]
+    return window.rearrange("n (j y) -> j n y", y=GROUP)[:, :, slack : slack + length]
+
+
 def tile_relativepositionsdpa_pa_s_kernel(tc, queries, v_bias, R, out):
     nc = tc.nc
     with tc.tile_pool(name="keep", bufs=1) as keep, tc.psum_pool(
-        name="transposed", bufs=4
-    ) as transposed, tc.psum_pool(name="scores", bufs=4) as scores:
+        name="transposed", bufs=3
+    ) as transposed, tc.psum_pool(name="scores", bufs=4) as scores, tc.psum_pool(name="leads", bufs=1) as leads:
         bias_rows = keep.tile([P, K // HALVES], BF16, name="bias_rows")
         nc.vector.memset(bias_rows[:], 0.0)
         nc.scalar.dma_start(
             out=bias_rows[0 : HEADS * HALVES, :],
             in_=v_bias.rearrange("o h i (u w) -> (o h i u) w", u=HALVES),
         )
-        q_raw = keep.tile([P, BATCHES, K], BF16, name="q_raw")
+        q_by_head = queries.rearrange("(n h) s k -> h s n k", h=HEADS)
+        q_raw = keep.tile([P, HEADS, SEQS, K], BF16, name="q_raw")
         r_raw = keep.tile([P, HEADS, CHUNKS, ROWS_EACH * K], BF16, name="r_raw")
         for h in range(HEADS):
+            nc.sync.dma_start(out=q_raw[:, h, :, :], in_=q_by_head[h])
             for c in range(CHUNKS):
                 nc.sync.dma_start(
                     out=r_raw[:, h, c, :],
                     in_=R[h, c * T_CHUNK : (c + 1) * T_CHUNK, :].rearrange("(r a) k -> r (a k)", a=ROWS_EACH),
                 )
-            for n in range(SEQS):
-                b = n * HEADS + h
-                nc.sync.dma_start(out=q_raw[:, b, :], in_=queries[b])
 
         identity = keep.tile([P, P], F32, name="identity")
         make_identity(nc, identity[:])
 
         padded = keep.tile([P, BATCHES, PITCH], F32, name="padded")
-        nc.gpsimd.memset(padded[:, :, 0 : LEAD + 1], 0.0)
+        nc.gpsimd.memset(padded[:, :, 0:BLOCK], 0.0)
 
-        q_grouped = keep.tile([P, BATCHES, S * PACK], BF16, name="q_grouped", align_bytes=64)
+        q_grouped = keep.tile([P, HEADS, 2, SEQS, S * PACK], BF16, name="q_grouped", align_bytes=64)
+        nc.vector.memset(q_grouped[:, :, 1, :, :], 0.0)
         r_grouped = keep.tile([P, HEADS, T * PACK], BF16, name="r_grouped", align_bytes=64)
-        q_codes = keep.tile([P, BATCHES, S], U32, name="q_codes", align_bytes=64)
-        q_scales = keep.tile([P, BATCHES, S], U8, name="q_scales", align_bytes=64)
+        q_codes = keep.tile([P, HEADS, 2, SEQS, S], U32, name="q_codes", align_bytes=64)
+        q_scales = keep.tile([P, HEADS, 2, SEQS, S], U8, name="q_scales", align_bytes=64)
         r_codes = keep.tile([P, HEADS, T], U32, name="r_codes", align_bytes=64)
         r_scales = keep.tile([P, HEADS, T], U8, name="r_scales", align_bytes=64)
 
@@ -73,8 +82,31 @@ def tile_relativepositionsdpa_pa_s_kernel(tc, queries, v_bias, R, out):
         nc.vector.tensor_copy(out=bias_words[:], in_=bias_t[:, 0 : HEADS * HALVES])
         bias_values = bias_words[:].bitcast(BF16)
 
+        out_flat = out.rearrange("(n h) s t -> n (h s t)", h=HEADS)
+
         for h in range(HEADS):
+            q_t = transposed.tile([P, SEQS, S, HALVES], F32, tag="t", name="q_t%d" % h)
+            for n in range(SEQS):
+                q_words = q_raw[:, h, n, :].bitcast(F32)
+                for u in range(HALVES):
+                    nc.tensor.transpose(q_t[:, n, :, u], q_words[:, u * P : (u + 1) * P], identity[:])
+            nc.vector.scalar_tensor_tensor(
+                out=q_grouped[:, h, 0, :, :].rearrange("p n (s t) -> p (n s) t", t=PACK),
+                in0=q_t[:].rearrange("p n s u -> p (n s u)").bitcast(BF16).rearrange("p (g t) -> p g t", t=PACK),
+                scalar=K**-0.5,
+                in1=bias_values[:, h * PACK : (h + 1) * PACK].unsqueeze(1).to_broadcast([P, SEQS * S, PACK]),
+                op0=MULT,
+                op1=ADD,
+            )
+            nc.vector.tensor_copy(out=q_grouped[:, h, 1, :, PACK:], in_=q_grouped[:, h, 0, :, : (S - 1) * PACK])
+            nc.vector.quantize_mx(
+                out=q_codes[:, h, :, :, :].rearrange("p v n s -> p (v n s)").bitcast(FP8X4),
+                scales=q_scales[:, h, :, :, :].rearrange("p v n s -> p (v n s)"),
+                in_=q_grouped[:, h, :, :, :].rearrange("p v n x -> p (v n x)"),
+            )
+
             for c in range(CHUNKS):
+                cols = slice(c * T_CHUNK, (c + 1) * T_CHUNK)
                 r_words = r_raw[:, h, c, :].bitcast(F32).rearrange("p (a u w) -> p a u w", a=ROWS_EACH, u=HALVES)
                 r_t = transposed.tile([P, ROWS_EACH, HALVES, P], F32, tag="t", name="r_t%d_%d" % (h, c))
                 for a in range(ROWS_EACH):
@@ -85,59 +117,51 @@ def tile_relativepositionsdpa_pa_s_kernel(tc, queries, v_bias, R, out):
                     out=piece.bitcast(F32).rearrange("p (r a u) -> p r a u", a=ROWS_EACH, u=HALVES),
                     in_=r_t[:].rearrange("p a u r -> p r a u"),
                 )
-                cols = slice(c * T_CHUNK, (c + 1) * T_CHUNK)
                 nc.vector.quantize_mx(
                     out=r_codes[:, h, cols].bitcast(FP8X4), scales=r_scales[:, h, cols], in_=piece
                 )
-            for n in range(SEQS):
-                b = n * HEADS + h
-                q_words = q_raw[:, b, :].bitcast(F32)
-                q_t = transposed.tile([P, S, HALVES], F32, tag="t", name="q_t%d" % b)
-                for u in range(HALVES):
-                    nc.tensor.transpose(q_t[:, :, u], q_words[:, u * P : (u + 1) * P], identity[:])
-                nc.vector.scalar_tensor_tensor(
-                    out=q_grouped[:, b, :].rearrange("p (s t) -> p s t", t=PACK),
-                    in0=q_t[:].rearrange("p s u -> p (s u)").bitcast(BF16).rearrange("p (s t) -> p s t", t=PACK),
-                    scalar=K**-0.5,
-                    in1=bias_values[:, h * PACK : (h + 1) * PACK].unsqueeze(1).to_broadcast([P, S, PACK]),
-                    op0=MULT,
-                    op1=ADD,
-                )
-                nc.vector.quantize_mx(
-                    out=q_codes[:, b, :].bitcast(FP8X4), scales=q_scales[:, b, :], in_=q_grouped[:, b, :]
-                )
-
-        for h in range(HEADS):
-            for n in range(SEQS):
-                b = n * HEADS + h
-                for c in range(CHUNKS):
-                    cols = slice(c * T_CHUNK, (c + 1) * T_CHUNK)
+                for n in range(SEQS):
+                    b = n * HEADS + h
                     pos = scores.tile([P, T_CHUNK], F32, tag="pos", name="pos%d_%d" % (b, c))
                     nc.tensor.matmul_mx(
                         out=pos[:],
-                        lhsT=q_codes[:, b, :].bitcast(FP8X4),
-                        lhsT_scale=q_scales[:, b, :],
+                        lhsT=q_codes[:, h, 0, n, :].bitcast(FP8X4),
+                        lhsT_scale=q_scales[:, h, 0, n, :],
                         rhs=r_codes[:, h, cols].bitcast(FP8X4),
                         rhs_scale=r_scales[:, h, cols],
                         start=True,
                         stop=True,
                     )
-                    first = LEAD + 1 + c * T_CHUNK
-                    if c == 0:
+                    first = BLOCK + c * T_CHUNK
+                    if n == 0:
                         nc.vector.tensor_copy(out=padded[:, b, first : first + T_CHUNK], in_=pos[:])
                     else:
                         nc.scalar.copy(out=padded[:, b, first : first + T_CHUNK], in_=pos[:])
-                flat = out[b].rearrange("s t -> (s t)")
-                split = SMALL_ROWS * PADDED - DROPPED
-                nc.sync.dma_start(
-                    out=flat[split:].rearrange("(s c) -> s c", c=PADDED),
-                    in_=padded[SMALL_ROWS:P, b, LEAD:PITCH],
+
+            lead = leads.tile([P, SEQS, LEAD_COLS], F32, tag="lead", name="lead%d" % h)
+            for n in range(SEQS):
+                nc.tensor.matmul_mx(
+                    out=lead[:, n, :],
+                    lhsT=q_codes[:, h, 1, n, :].bitcast(FP8X4),
+                    lhsT_scale=q_scales[:, h, 1, n, :],
+                    rhs=r_codes[:, h, T - LEAD_COLS : T].bitcast(FP8X4),
+                    rhs_scale=r_scales[:, h, T - LEAD_COLS : T],
+                    start=True,
+                    stop=True,
                 )
-                nc.sync.dma_start(
-                    out=flat[PADDED - DROPPED : split].rearrange("(s c) -> s c", c=PADDED),
-                    in_=padded[1:SMALL_ROWS, b, LEAD:PITCH],
+            nc.scalar.copy(out=padded[:, h::HEADS, 0:LEAD], in_=lead[:, :, LEAD_COLS - LEAD :])
+
+            origin = h * S * T - DROPPED
+            for r in (0, 4, 1, 5, 2, 6, 3, 7):
+                length = T if r < BLOCK - 1 else T + BLOCK
+                skipped = 1 if r == 0 else 0
+                queue = nc.sync if r < BLOCK // 2 else nc.scalar
+                queue.dma_start(
+                    out=runs_a_group_apart(out_flat, origin + skipped * GROUP + r * T, GROUPS - skipped, length),
+                    in_=padded[skipped * BLOCK + r : P : BLOCK, h::HEADS, LEAD - r : LEAD - r + length],
                 )
-                nc.sync.dma_start(
-                    out=flat[0 : PADDED - DROPPED].unsqueeze(0),
-                    in_=padded[0:1, b, LEAD + DROPPED : PITCH],
-                )
+
+        nc.gpsimd.dma_start(
+            out=out.rearrange("b s t -> b (s t)")[:, 0 : T - DROPPED].unsqueeze(0),
+            in_=padded[0:1, :, LEAD + DROPPED : LEAD + T],
+        )

@@ -22,29 +22,37 @@ T_CHUNK = 256
 CHUNKS = T // T_CHUNK
 ROWS_EACH = T_CHUNK // P
 PADDED = T + 1
+PITCH = 520
 DROPPED = S
-BLOCK = 8
-LEAD = BLOCK - 1
-PITCH = LEAD + PADDED
-GROUP = BLOCK * PADDED
-GROUPS = S // BLOCK
-LEAD_COLS = 128
+LARGE = 16
+WARM_PASSES = 5
 
 FLOPS = 2 * BATCHES * S * T * K
 BYTES = 2 * (BATCHES * S * K + HEADS * K + HEADS * T * K) + 4 * BATCHES * S * T
 
 
-def runs_a_group_apart(flat, first, count, length):
-    slack = min(first, GROUP - length)
-    window = flat[:, first - slack : first - slack + count * GROUP]
-    return window.rearrange("n (j y) -> j n y", y=GROUP)[:, :, slack : slack + length]
-
-
 def tile_relativepositionsdpa_pa_s_kernel(tc, queries, v_bias, R, out):
     nc = tc.nc
     with tc.tile_pool(name="keep", bufs=1) as keep, tc.psum_pool(
-        name="transposed", bufs=3
-    ) as transposed, tc.psum_pool(name="scores", bufs=4) as scores, tc.psum_pool(name="leads", bufs=1) as leads:
+        name="transposed", bufs=4
+    ) as transposed, tc.psum_pool(name="scores", bufs=4) as scores:
+        warm_values = keep.tile([P, T * PACK], BF16, name="warm_values", align_bytes=64)
+        warm_codes = keep.tile([P, T], U32, name="warm_codes", align_bytes=64)
+        warm_scales = keep.tile([P, T], U8, name="warm_scales", align_bytes=64)
+        nc.vector.memset(warm_values[:], 0.0)
+        nc.vector.quantize_mx(out=warm_codes[:].bitcast(FP8X4), scales=warm_scales[:], in_=warm_values[:])
+        warm = scores.tile([P, T], F32, tag="pos", name="warm")
+        for i in range(WARM_PASSES):
+            nc.tensor.matmul_mx(
+                out=warm[:],
+                lhsT=warm_codes[:, 0:S].bitcast(FP8X4),
+                lhsT_scale=warm_scales[:, 0:S],
+                rhs=warm_codes[:].bitcast(FP8X4),
+                rhs_scale=warm_scales[:],
+                start=True,
+                stop=True,
+            )
+
         bias_rows = keep.tile([P, K // HALVES], BF16, name="bias_rows")
         nc.vector.memset(bias_rows[:], 0.0)
         nc.scalar.dma_start(
@@ -66,13 +74,12 @@ def tile_relativepositionsdpa_pa_s_kernel(tc, queries, v_bias, R, out):
         make_identity(nc, identity[:])
 
         padded = keep.tile([P, BATCHES, PITCH], F32, name="padded")
-        nc.gpsimd.memset(padded[:, :, 0:BLOCK], 0.0)
+        nc.gpsimd.memset(padded[:, :, 0:8], 0.0)
 
-        q_grouped = keep.tile([P, HEADS, 2, SEQS, S * PACK], BF16, name="q_grouped", align_bytes=64)
-        nc.vector.memset(q_grouped[:, :, 1, :, :], 0.0)
+        q_grouped = keep.tile([P, HEADS, SEQS * S, PACK], BF16, name="q_grouped", align_bytes=64)
         r_grouped = keep.tile([P, HEADS, T * PACK], BF16, name="r_grouped", align_bytes=64)
-        q_codes = keep.tile([P, HEADS, 2, SEQS, S], U32, name="q_codes", align_bytes=64)
-        q_scales = keep.tile([P, HEADS, 2, SEQS, S], U8, name="q_scales", align_bytes=64)
+        q_codes = keep.tile([P, HEADS, SEQS, S], U32, name="q_codes", align_bytes=64)
+        q_scales = keep.tile([P, HEADS, SEQS, S], U8, name="q_scales", align_bytes=64)
         r_codes = keep.tile([P, HEADS, T], U32, name="r_codes", align_bytes=64)
         r_scales = keep.tile([P, HEADS, T], U8, name="r_scales", align_bytes=64)
 
@@ -82,27 +89,36 @@ def tile_relativepositionsdpa_pa_s_kernel(tc, queries, v_bias, R, out):
         nc.vector.tensor_copy(out=bias_words[:], in_=bias_t[:, 0 : HEADS * HALVES])
         bias_values = bias_words[:].bitcast(BF16)
 
-        out_flat = out.rearrange("(n h) s t -> n (h s t)", h=HEADS)
+        out_flat = out.rearrange("b s t -> b (s t)")
+
+        def store_rows(first, batches):
+            nc.sync.dma_start(
+                out=out_flat[batches, first * PADDED - DROPPED : 2 * first * PADDED - DROPPED].rearrange(
+                    "b (s c) -> s b c", c=PADDED
+                ),
+                in_=padded[first : 2 * first, batches, 0:PADDED],
+            )
 
         for h in range(HEADS):
-            q_t = transposed.tile([P, SEQS, S, HALVES], F32, tag="t", name="q_t%d" % h)
+            q_t = transposed.tile([P, HALVES, SEQS, S], F32, tag="t", name="q_t%d" % h)
             for n in range(SEQS):
                 q_words = q_raw[:, h, n, :].bitcast(F32)
                 for u in range(HALVES):
-                    nc.tensor.transpose(q_t[:, n, :, u], q_words[:, u * P : (u + 1) * P], identity[:])
-            nc.vector.scalar_tensor_tensor(
-                out=q_grouped[:, h, 0, :, :].rearrange("p n (s t) -> p (n s) t", t=PACK),
-                in0=q_t[:].rearrange("p n s u -> p (n s u)").bitcast(BF16).rearrange("p (g t) -> p g t", t=PACK),
-                scalar=K**-0.5,
-                in1=bias_values[:, h * PACK : (h + 1) * PACK].unsqueeze(1).to_broadcast([P, SEQS * S, PACK]),
-                op0=MULT,
-                op1=ADD,
-            )
-            nc.vector.tensor_copy(out=q_grouped[:, h, 1, :, PACK:], in_=q_grouped[:, h, 0, :, : (S - 1) * PACK])
+                    nc.tensor.transpose(q_t[:, u, n, :], q_words[:, u * P : (u + 1) * P], identity[:])
+            for u in range(HALVES):
+                first = h * PACK + u * 2
+                nc.vector.scalar_tensor_tensor(
+                    out=q_grouped[:, h, :, u * 2 : u * 2 + 2],
+                    in0=q_t[:, u, :, :].rearrange("p n s -> p (n s)").bitcast(BF16).rearrange("p (g e) -> p g e", e=2),
+                    scalar=K**-0.5,
+                    in1=bias_values[:, first : first + 2].unsqueeze(1).to_broadcast([P, SEQS * S, 2]),
+                    op0=MULT,
+                    op1=ADD,
+                )
             nc.vector.quantize_mx(
-                out=q_codes[:, h, :, :, :].rearrange("p v n s -> p (v n s)").bitcast(FP8X4),
-                scales=q_scales[:, h, :, :, :].rearrange("p v n s -> p (v n s)"),
-                in_=q_grouped[:, h, :, :, :].rearrange("p v n x -> p (v n x)"),
+                out=q_codes[:, h, :, :].rearrange("p n s -> p (n s)").bitcast(FP8X4),
+                scales=q_scales[:, h, :, :].rearrange("p n s -> p (n s)"),
+                in_=q_grouped[:, h, :, :].rearrange("p g t -> p (g t)"),
             )
 
             for c in range(CHUNKS):
@@ -125,43 +141,25 @@ def tile_relativepositionsdpa_pa_s_kernel(tc, queries, v_bias, R, out):
                     pos = scores.tile([P, T_CHUNK], F32, tag="pos", name="pos%d_%d" % (b, c))
                     nc.tensor.matmul_mx(
                         out=pos[:],
-                        lhsT=q_codes[:, h, 0, n, :].bitcast(FP8X4),
-                        lhsT_scale=q_scales[:, h, 0, n, :],
+                        lhsT=q_codes[:, h, n, :].bitcast(FP8X4),
+                        lhsT_scale=q_scales[:, h, n, :],
                         rhs=r_codes[:, h, cols].bitcast(FP8X4),
                         rhs_scale=r_scales[:, h, cols],
                         start=True,
                         stop=True,
                     )
-                    first = BLOCK + c * T_CHUNK
+                    first = 1 + c * T_CHUNK
                     if n == 0:
                         nc.vector.tensor_copy(out=padded[:, b, first : first + T_CHUNK], in_=pos[:])
                     else:
                         nc.scalar.copy(out=padded[:, b, first : first + T_CHUNK], in_=pos[:])
 
-            lead = leads.tile([P, SEQS, LEAD_COLS], F32, tag="lead", name="lead%d" % h)
-            for n in range(SEQS):
-                nc.tensor.matmul_mx(
-                    out=lead[:, n, :],
-                    lhsT=q_codes[:, h, 1, n, :].bitcast(FP8X4),
-                    lhsT_scale=q_scales[:, h, 1, n, :],
-                    rhs=r_codes[:, h, T - LEAD_COLS : T].bitcast(FP8X4),
-                    rhs_scale=r_scales[:, h, T - LEAD_COLS : T],
-                    start=True,
-                    stop=True,
-                )
-            nc.scalar.copy(out=padded[:, h::HEADS, 0:LEAD], in_=lead[:, :, LEAD_COLS - LEAD :])
+            for first in (64, 32, 16):
+                store_rows(first, slice(h, BATCHES, HEADS))
 
-            origin = h * S * T - DROPPED
-            for r in (0, 4, 1, 5, 2, 6, 3, 7):
-                length = T if r < BLOCK - 1 else T + BLOCK
-                skipped = 1 if r == 0 else 0
-                queue = nc.sync if r < BLOCK // 2 else nc.scalar
-                queue.dma_start(
-                    out=runs_a_group_apart(out_flat, origin + skipped * GROUP + r * T, GROUPS - skipped, length),
-                    in_=padded[skipped * BLOCK + r : P : BLOCK, h::HEADS, LEAD - r : LEAD - r + length],
-                )
-
-        nc.gpsimd.dma_start(
-            out=out.rearrange("b s t -> b (s t)")[:, 0 : T - DROPPED].unsqueeze(0),
-            in_=padded[0:1, :, LEAD + DROPPED : LEAD + T],
+        for first in (8, 4, 2, 1):
+            store_rows(first, slice(0, BATCHES))
+        nc.sync.dma_start(
+            out=out_flat[:, 0 : PADDED - DROPPED].unsqueeze(0),
+            in_=padded[0:1, :, DROPPED:PADDED],
         )

@@ -24,8 +24,8 @@ ROWS_EACH = T_CHUNK // P
 PADDED = T + 1
 PITCH = 520
 DROPPED = S
-LARGE = 16
-WARM_PASSES = 5
+SMALL_ROWS = 16
+WARM_PASSES = 16
 
 FLOPS = 2 * BATCHES * S * T * K
 BYTES = 2 * (BATCHES * S * K + HEADS * K + HEADS * T * K) + 4 * BATCHES * S * T
@@ -36,26 +36,9 @@ def tile_relativepositionsdpa_pa_s_kernel(tc, queries, v_bias, R, out):
     with tc.tile_pool(name="keep", bufs=1) as keep, tc.psum_pool(
         name="transposed", bufs=4
     ) as transposed, tc.psum_pool(name="scores", bufs=4) as scores:
-        warm_values = keep.tile([P, T * PACK], BF16, name="warm_values", align_bytes=64)
-        warm_codes = keep.tile([P, T], U32, name="warm_codes", align_bytes=64)
-        warm_scales = keep.tile([P, T], U8, name="warm_scales", align_bytes=64)
-        nc.vector.memset(warm_values[:], 0.0)
-        nc.vector.quantize_mx(out=warm_codes[:].bitcast(FP8X4), scales=warm_scales[:], in_=warm_values[:])
-        warm = scores.tile([P, T], F32, tag="pos", name="warm")
-        for i in range(WARM_PASSES):
-            nc.tensor.matmul_mx(
-                out=warm[:],
-                lhsT=warm_codes[:, 0:S].bitcast(FP8X4),
-                lhsT_scale=warm_scales[:, 0:S],
-                rhs=warm_codes[:].bitcast(FP8X4),
-                rhs_scale=warm_scales[:],
-                start=True,
-                stop=True,
-            )
-
         bias_rows = keep.tile([P, K // HALVES], BF16, name="bias_rows")
         nc.vector.memset(bias_rows[:], 0.0)
-        nc.scalar.dma_start(
+        nc.sync.dma_start(
             out=bias_rows[0 : HEADS * HALVES, :],
             in_=v_bias.rearrange("o h i (u w) -> (o h i u) w", u=HALVES),
         )
@@ -72,6 +55,23 @@ def tile_relativepositionsdpa_pa_s_kernel(tc, queries, v_bias, R, out):
 
         identity = keep.tile([P, P], F32, name="identity")
         make_identity(nc, identity[:])
+
+        warm_values = keep.tile([P, S * PACK], BF16, name="warm_values", align_bytes=64)
+        warm_codes = keep.tile([P, S], U32, name="warm_codes", align_bytes=64)
+        warm_scales = keep.tile([P, S], U8, name="warm_scales", align_bytes=64)
+        nc.vector.memset(warm_values[:], 0.0)
+        nc.vector.quantize_mx(out=warm_codes[:].bitcast(FP8X4), scales=warm_scales[:], in_=warm_values[:])
+        warm = scores.tile([P, S], F32, tag="pos", name="warm")
+        for i in range(WARM_PASSES):
+            nc.tensor.matmul_mx(
+                out=warm[:],
+                lhsT=warm_codes[:].bitcast(FP8X4),
+                lhsT_scale=warm_scales[:],
+                rhs=warm_codes[:].bitcast(FP8X4),
+                rhs_scale=warm_scales[:],
+                start=True,
+                stop=True,
+            )
 
         padded = keep.tile([P, BATCHES, PITCH], F32, name="padded")
         nc.gpsimd.memset(padded[:, :, 0:8], 0.0)
@@ -91,12 +91,12 @@ def tile_relativepositionsdpa_pa_s_kernel(tc, queries, v_bias, R, out):
 
         out_flat = out.rearrange("b s t -> b (s t)")
 
-        def store_rows(first, batches):
+        def store_rows(first, end, batches):
             nc.sync.dma_start(
-                out=out_flat[batches, first * PADDED - DROPPED : 2 * first * PADDED - DROPPED].rearrange(
+                out=out_flat[batches, first * PADDED - DROPPED : end * PADDED - DROPPED].rearrange(
                     "b (s c) -> s b c", c=PADDED
                 ),
-                in_=padded[first : 2 * first, batches, 0:PADDED],
+                in_=padded[first:end, batches, 0:PADDED],
             )
 
         for h in range(HEADS):
@@ -154,11 +154,9 @@ def tile_relativepositionsdpa_pa_s_kernel(tc, queries, v_bias, R, out):
                     else:
                         nc.scalar.copy(out=padded[:, b, first : first + T_CHUNK], in_=pos[:])
 
-            for first in (64, 32, 16):
-                store_rows(first, slice(h, BATCHES, HEADS))
+            store_rows(SMALL_ROWS, S, slice(h, BATCHES, HEADS))
 
-        for first in (8, 4, 2, 1):
-            store_rows(first, slice(0, BATCHES))
+        store_rows(1, SMALL_ROWS, slice(0, BATCHES))
         nc.sync.dma_start(
             out=out_flat[:, 0 : PADDED - DROPPED].unsqueeze(0),
             in_=padded[0:1, :, DROPPED:PADDED],

@@ -49,8 +49,8 @@ def tile_relativepositionsdpa_pa_s_kernel(tc, queries, v_bias, R, out):
             nc.sync.dma_start(out=q_raw[:, h, :, :], in_=q_by_head[h])
             for c in range(CHUNKS):
                 nc.sync.dma_start(
-                    out=r_raw[:, h, c, :],
-                    in_=R[h, c * T_CHUNK : (c + 1) * T_CHUNK, :].rearrange("(r a) k -> r (a k)", a=ROWS_EACH),
+                    out=r_raw[:, h, c, :].rearrange("p (a k) -> p a k", a=ROWS_EACH),
+                    in_=R[h, c * T_CHUNK : (c + 1) * T_CHUNK, :].rearrange("(a r) k -> r a k", a=ROWS_EACH),
                 )
 
         identity = keep.tile([P, P], F32, name="identity")
@@ -130,8 +130,8 @@ def tile_relativepositionsdpa_pa_s_kernel(tc, queries, v_bias, R, out):
                         nc.tensor.transpose(r_t[:, a, u, :], r_words[:, a, u, :], identity[:])
                 piece = r_grouped[:, h, c * T_CHUNK * PACK : (c + 1) * T_CHUNK * PACK]
                 nc.scalar.copy(
-                    out=piece.bitcast(F32).rearrange("p (r a u) -> p r a u", a=ROWS_EACH, u=HALVES),
-                    in_=r_t[:].rearrange("p a u r -> p r a u"),
+                    out=piece.bitcast(F32).rearrange("p (a r u) -> p a r u", a=ROWS_EACH, u=HALVES),
+                    in_=r_t[:].rearrange("p a u r -> p a r u"),
                 )
                 nc.vector.quantize_mx(
                     out=r_codes[:, h, cols].bitcast(FP8X4), scales=r_scales[:, h, cols], in_=piece

@@ -25,7 +25,6 @@ PADDED = T + 1
 PITCH = 520
 DROPPED = S
 SMALL_ROWS = 16
-WARM_PASSES = 16
 
 FLOPS = 2 * BATCHES * S * T * K
 BYTES = 2 * (BATCHES * S * K + HEADS * K + HEADS * T * K) + 4 * BATCHES * S * T
@@ -56,22 +55,6 @@ def tile_relativepositionsdpa_pa_s_kernel(tc, queries, v_bias, R, out):
         identity = keep.tile([P, P], F32, name="identity")
         make_identity(nc, identity[:])
 
-        warm_values = keep.tile([P, S * PACK], BF16, name="warm_values", align_bytes=64)
-        warm_codes = keep.tile([P, S], U32, name="warm_codes", align_bytes=64)
-        warm_scales = keep.tile([P, S], U8, name="warm_scales", align_bytes=64)
-        nc.vector.memset(warm_values[:], 0.0)
-        nc.vector.quantize_mx(out=warm_codes[:].bitcast(FP8X4), scales=warm_scales[:], in_=warm_values[:])
-        warm = scores.tile([P, S], F32, tag="pos", name="warm")
-        for i in range(WARM_PASSES):
-            nc.tensor.matmul_mx(
-                out=warm[:],
-                lhsT=warm_codes[:].bitcast(FP8X4),
-                lhsT_scale=warm_scales[:],
-                rhs=warm_codes[:].bitcast(FP8X4),
-                rhs_scale=warm_scales[:],
-                start=True,
-                stop=True,
-            )
 
         padded = keep.tile([P, BATCHES, PITCH], F32, name="padded")
         nc.gpsimd.memset(padded[:, :, 0:8], 0.0)
@@ -154,10 +137,10 @@ def tile_relativepositionsdpa_pa_s_kernel(tc, queries, v_bias, R, out):
                     else:
                         nc.scalar.copy(out=padded[:, b, first : first + T_CHUNK], in_=pos[:])
 
-            store_rows(SMALL_ROWS, S, slice(h, BATCHES, HEADS))
-
-        store_rows(1, SMALL_ROWS, slice(0, BATCHES))
-        nc.sync.dma_start(
-            out=out_flat[:, 0 : PADDED - DROPPED].unsqueeze(0),
-            in_=padded[0:1, :, DROPPED:PADDED],
-        )
+            of_head = slice(h, BATCHES, HEADS)
+            store_rows(SMALL_ROWS, S, of_head)
+            store_rows(1, SMALL_ROWS, of_head)
+            nc.sync.dma_start(
+                out=out_flat[of_head, 0 : PADDED - DROPPED].unsqueeze(0),
+                in_=padded[0:1, of_head, DROPPED:PADDED],
+            )

@@ -22,9 +22,12 @@ T_CHUNK = 256
 CHUNKS = T // T_CHUNK
 ROWS_EACH = T_CHUNK // P
 PADDED = T + 1
-PITCH = 520
 DROPPED = S
-SMALL_ROWS = 16
+PAIR = 2
+PAIRS = S // PAIR
+FRONT = 6
+PITCH = FRONT + PAIR * PADDED
+SMALL_PAIRS = 16
 
 FLOPS = 2 * BATCHES * S * T * K
 BYTES = 2 * (BATCHES * S * K + HEADS * K + HEADS * T * K) + 4 * BATCHES * S * T
@@ -56,13 +59,14 @@ def tile_relativepositionsdpa_pa_s_kernel(tc, queries, v_bias, R, out):
         make_identity(nc, identity[:])
 
 
-        padded = keep.tile([P, BATCHES, PITCH], F32, name="padded")
-        nc.gpsimd.memset(padded[:, :, 0:8], 0.0)
+        paired = keep.tile([P, HEADS, PITCH], F32, name="paired")
+        nc.gpsimd.memset(paired[:, :, 0:8], 0.0)
+        nc.gpsimd.memset(paired[:, :, FRONT + PADDED - 7 : FRONT + PADDED + 1], 0.0)
 
-        q_grouped = keep.tile([P, HEADS, SEQS * S, PACK], BF16, name="q_grouped", align_bytes=64)
+        q_grouped = keep.tile([P, HEADS, PAIR, SEQS * PAIRS, PACK], BF16, name="q_grouped", align_bytes=64)
         r_grouped = keep.tile([P, HEADS, T * PACK], BF16, name="r_grouped", align_bytes=64)
-        q_codes = keep.tile([P, HEADS, SEQS, S], U32, name="q_codes", align_bytes=64)
-        q_scales = keep.tile([P, HEADS, SEQS, S], U8, name="q_scales", align_bytes=64)
+        q_codes = keep.tile([P, HEADS, PAIR, SEQS * PAIRS], U32, name="q_codes", align_bytes=64)
+        q_scales = keep.tile([P, HEADS, PAIR, SEQS * PAIRS], U8, name="q_scales", align_bytes=64)
         r_codes = keep.tile([P, HEADS, T], U32, name="r_codes", align_bytes=64)
         r_scales = keep.tile([P, HEADS, T], U8, name="r_scales", align_bytes=64)
 
@@ -74,12 +78,12 @@ def tile_relativepositionsdpa_pa_s_kernel(tc, queries, v_bias, R, out):
 
         out_flat = out.rearrange("b s t -> b (s t)")
 
-        def store_rows(first, end, batches):
+        def store_pairs(first, end, n, h):
             nc.sync.dma_start(
-                out=out_flat[batches, first * PADDED - DROPPED : end * PADDED - DROPPED].rearrange(
-                    "b (s c) -> s b c", c=PADDED
-                ),
-                in_=padded[first:end, batches, 0:PADDED],
+                out=out_flat[
+                    n * HEADS + h, first * PAIR * PADDED - DROPPED : end * PAIR * PADDED - DROPPED
+                ].rearrange("(m c) -> m c", c=PAIR * PADDED),
+                in_=paired[n * PAIRS + first : n * PAIRS + end, h, FRONT:PITCH],
             )
 
         for h in range(HEADS):
@@ -90,18 +94,22 @@ def tile_relativepositionsdpa_pa_s_kernel(tc, queries, v_bias, R, out):
                     nc.tensor.transpose(q_t[:, u, n, :], q_words[:, u * P : (u + 1) * P], identity[:])
             for u in range(HALVES):
                 first = h * PACK + u * 2
-                nc.vector.scalar_tensor_tensor(
-                    out=q_grouped[:, h, :, u * 2 : u * 2 + 2],
-                    in0=q_t[:, u, :, :].rearrange("p n s -> p (n s)").bitcast(BF16).rearrange("p (g e) -> p g e", e=2),
-                    scalar=K**-0.5,
-                    in1=bias_values[:, first : first + 2].unsqueeze(1).to_broadcast([P, SEQS * S, 2]),
-                    op0=MULT,
-                    op1=ADD,
+                q_pairs = q_t[:, u, :, :].rearrange("p n s -> p (n s)").bitcast(BF16).rearrange(
+                    "p (g w e) -> p g w e", w=PAIR, e=2
                 )
+                for w in range(PAIR):
+                    nc.vector.scalar_tensor_tensor(
+                        out=q_grouped[:, h, w, :, u * 2 : u * 2 + 2],
+                        in0=q_pairs[:, :, w, :],
+                        scalar=K**-0.5,
+                        in1=bias_values[:, first : first + 2].unsqueeze(1).to_broadcast([P, SEQS * PAIRS, 2]),
+                        op0=MULT,
+                        op1=ADD,
+                    )
             nc.vector.quantize_mx(
-                out=q_codes[:, h, :, :].rearrange("p n s -> p (n s)").bitcast(FP8X4),
-                scales=q_scales[:, h, :, :].rearrange("p n s -> p (n s)"),
-                in_=q_grouped[:, h, :, :].rearrange("p g t -> p (g t)"),
+                out=q_codes[:, h, :, :].rearrange("p w g -> p (w g)").bitcast(FP8X4),
+                scales=q_scales[:, h, :, :].rearrange("p w g -> p (w g)"),
+                in_=q_grouped[:, h, :, :, :].rearrange("p w g t -> p (w g t)"),
             )
 
             for c in range(CHUNKS):
@@ -119,28 +127,28 @@ def tile_relativepositionsdpa_pa_s_kernel(tc, queries, v_bias, R, out):
                 nc.vector.quantize_mx(
                     out=r_codes[:, h, cols].bitcast(FP8X4), scales=r_scales[:, h, cols], in_=piece
                 )
-                for n in range(SEQS):
-                    b = n * HEADS + h
-                    pos = scores.tile([P, T_CHUNK], F32, tag="pos", name="pos%d_%d" % (b, c))
+                for w in range(PAIR):
+                    pos = scores.tile([P, T_CHUNK], F32, tag="pos", name="pos%d_%d_%d" % (h, c, w))
                     nc.tensor.matmul_mx(
                         out=pos[:],
-                        lhsT=q_codes[:, h, n, :].bitcast(FP8X4),
-                        lhsT_scale=q_scales[:, h, n, :],
+                        lhsT=q_codes[:, h, w, :].bitcast(FP8X4),
+                        lhsT_scale=q_scales[:, h, w, :],
                         rhs=r_codes[:, h, cols].bitcast(FP8X4),
                         rhs_scale=r_scales[:, h, cols],
                         start=True,
                         stop=True,
                     )
-                    first = 1 + c * T_CHUNK
-                    if n == 0:
-                        nc.vector.tensor_copy(out=padded[:, b, first : first + T_CHUNK], in_=pos[:])
+                    first = FRONT + w * PADDED + 1 + c * T_CHUNK
+                    if w == 0:
+                        nc.vector.tensor_copy(out=paired[:, h, first : first + T_CHUNK], in_=pos[:])
                     else:
-                        nc.scalar.copy(out=padded[:, b, first : first + T_CHUNK], in_=pos[:])
+                        nc.scalar.copy(out=paired[:, h, first : first + T_CHUNK], in_=pos[:])
 
-            of_head = slice(h, BATCHES, HEADS)
-            store_rows(SMALL_ROWS, S, of_head)
-            store_rows(1, SMALL_ROWS, of_head)
-            nc.sync.dma_start(
-                out=out_flat[of_head, 0 : PADDED - DROPPED].unsqueeze(0),
-                in_=padded[0:1, of_head, DROPPED:PADDED],
-            )
+            for n in range(SEQS):
+                store_pairs(SMALL_PAIRS, PAIRS, n, h)
+            for n in range(SEQS):
+                store_pairs(1, SMALL_PAIRS, n, h)
+                nc.sync.dma_start(
+                    out=out_flat[n * HEADS + h, 0 : PAIR * PADDED - DROPPED].unsqueeze(0),
+                    in_=paired[n * PAIRS : n * PAIRS + 1, h, FRONT + DROPPED : PITCH],
+                )

import concourse.mybir as mybir
from concourse.masks import make_identity

F32 = mybir.dt.float32
BF16 = mybir.dt.bfloat16
U32 = mybir.dt.uint32
U8 = mybir.dt.uint8
FP8X4 = mybir.dt.float8_e4m3fn_x4
MULT = mybir.AluOpType.mult
ADD = mybir.AluOpType.add

P = 128
SEQS = 2
HEADS = 2
BATCHES = SEQS * HEADS
S = 128
T = 512
K = 512
PACK = 4
HALVES = 2
T_CHUNK = 256
CHUNKS = T // T_CHUNK
ROWS_EACH = T_CHUNK // P
PADDED = T + 1
DROPPED = S
PAIR = 2
PAIRS = S // PAIR
FRONT = 6
PITCH = FRONT + PAIR * PADDED
SMALL_PAIRS = 16

FLOPS = 2 * BATCHES * S * T * K
BYTES = 2 * (BATCHES * S * K + HEADS * K + HEADS * T * K) + 4 * BATCHES * S * T


def tile_relativepositionsdpa_pa_s_kernel(tc, queries, v_bias, R, out):
    nc = tc.nc
    with tc.tile_pool(name="keep", bufs=1) as keep, tc.psum_pool(
        name="transposed", bufs=4
    ) as transposed, tc.psum_pool(name="scores", bufs=4) as scores:
        bias_rows = keep.tile([P, K // HALVES], BF16, name="bias_rows")
        nc.vector.memset(bias_rows[:], 0.0)
        nc.sync.dma_start(
            out=bias_rows[0 : HEADS * HALVES, :],
            in_=v_bias.rearrange("o h i (u w) -> (o h i u) w", u=HALVES),
        )
        q_by_head = queries.rearrange("(n h) s k -> h s n k", h=HEADS)
        q_raw = keep.tile([P, HEADS, SEQS, K], BF16, name="q_raw")
        r_raw = keep.tile([P, HEADS, CHUNKS, ROWS_EACH * K], BF16, name="r_raw")
        for h in range(HEADS):
            nc.sync.dma_start(out=q_raw[:, h, :, :], in_=q_by_head[h])
            for c in range(CHUNKS):
                nc.sync.dma_start(
                    out=r_raw[:, h, c, :].rearrange("p (a k) -> p a k", a=ROWS_EACH),
                    in_=R[h, c * T_CHUNK : (c + 1) * T_CHUNK, :].rearrange("(a r) k -> r a k", a=ROWS_EACH),
                )

        identity = keep.tile([P, P], F32, name="identity")
        make_identity(nc, identity[:])


        paired = keep.tile([P, HEADS, PITCH], F32, name="paired")
        nc.gpsimd.memset(paired[:, :, 0:8], 0.0)
        nc.gpsimd.memset(paired[:, :, FRONT + PADDED - 7 : FRONT + PADDED + 1], 0.0)

        q_grouped = keep.tile([P, HEADS, PAIR, SEQS * PAIRS, PACK], BF16, name="q_grouped", align_bytes=64)
        r_grouped = keep.tile([P, HEADS, T * PACK], BF16, name="r_grouped", align_bytes=64)
        q_codes = keep.tile([P, HEADS, PAIR, SEQS * PAIRS], U32, name="q_codes", align_bytes=64)
        q_scales = keep.tile([P, HEADS, PAIR, SEQS * PAIRS], U8, name="q_scales", align_bytes=64)
        r_codes = keep.tile([P, HEADS, T], U32, name="r_codes", align_bytes=64)
        r_scales = keep.tile([P, HEADS, T], U8, name="r_scales", align_bytes=64)

        bias_t = transposed.tile([P, P], F32, tag="t", name="bias_t")
        nc.tensor.transpose(bias_t[:], bias_rows[:].bitcast(F32), identity[:])
        bias_words = keep.tile([P, HEADS * HALVES], F32, name="bias_words")
        nc.vector.tensor_copy(out=bias_words[:], in_=bias_t[:, 0 : HEADS * HALVES])
        bias_values = bias_words[:].bitcast(BF16)

        out_flat = out.rearrange("b s t -> b (s t)")

        def store_pairs(first, end, n, h):
            nc.sync.dma_start(
                out=out_flat[
                    n * HEADS + h, first * PAIR * PADDED - DROPPED : end * PAIR * PADDED - DROPPED
                ].rearrange("(m c) -> m c", c=PAIR * PADDED),
                in_=paired[n * PAIRS + first : n * PAIRS + end, h, FRONT:PITCH],
            )

        for h in range(HEADS):
            q_t = transposed.tile([P, HALVES, SEQS, S], F32, tag="t", name="q_t%d" % h)
            for n in range(SEQS):
                q_words = q_raw[:, h, n, :].bitcast(F32)
                for u in range(HALVES):
                    nc.tensor.transpose(q_t[:, u, n, :], q_words[:, u * P : (u + 1) * P], identity[:])
            for u in range(HALVES):
                first = h * PACK + u * 2
                q_pairs = q_t[:, u, :, :].rearrange("p n s -> p (n s)").bitcast(BF16).rearrange(
                    "p (g w e) -> p g w e", w=PAIR, e=2
                )
                for w in range(PAIR):
                    nc.vector.scalar_tensor_tensor(
                        out=q_grouped[:, h, w, :, u * 2 : u * 2 + 2],
                        in0=q_pairs[:, :, w, :],
                        scalar=K**-0.5,
                        in1=bias_values[:, first : first + 2].unsqueeze(1).to_broadcast([P, SEQS * PAIRS, 2]),
                        op0=MULT,
                        op1=ADD,
                    )
            nc.vector.quantize_mx(
                out=q_codes[:, h, :, :].rearrange("p w g -> p (w g)").bitcast(FP8X4),
                scales=q_scales[:, h, :, :].rearrange("p w g -> p (w g)"),
                in_=q_grouped[:, h, :, :, :].rearrange("p w g t -> p (w g t)"),
            )

            for c in range(CHUNKS):
                cols = slice(c * T_CHUNK, (c + 1) * T_CHUNK)
                r_words = r_raw[:, h, c, :].bitcast(F32).rearrange("p (a u w) -> p a u w", a=ROWS_EACH, u=HALVES)
                r_t = transposed.tile([P, ROWS_EACH, HALVES, P], F32, tag="t", name="r_t%d_%d" % (h, c))
                for a in range(ROWS_EACH):
                    for u in range(HALVES):
                        nc.tensor.transpose(r_t[:, a, u, :], r_words[:, a, u, :], identity[:])
                piece = r_grouped[:, h, c * T_CHUNK * PACK : (c + 1) * T_CHUNK * PACK]
                nc.scalar.copy(
                    out=piece.bitcast(F32).rearrange("p (a r u) -> p a r u", a=ROWS_EACH, u=HALVES),
                    in_=r_t[:].rearrange("p a u r -> p a r u"),
                )
                nc.vector.quantize_mx(
                    out=r_codes[:, h, cols].bitcast(FP8X4), scales=r_scales[:, h, cols], in_=piece
                )
                for w in range(PAIR):
                    pos = scores.tile([P, T_CHUNK], F32, tag="pos", name="pos%d_%d_%d" % (h, c, w))
                    nc.tensor.matmul_mx(
                        out=pos[:],
                        lhsT=q_codes[:, h, w, :].bitcast(FP8X4),
                        lhsT_scale=q_scales[:, h, w, :],
                        rhs=r_codes[:, h, cols].bitcast(FP8X4),
                        rhs_scale=r_scales[:, h, cols],
                        start=True,
                        stop=True,
                    )
                    first = FRONT + w * PADDED + 1 + c * T_CHUNK
                    if w == 0:
                        nc.vector.tensor_copy(out=paired[:, h, first : first + T_CHUNK], in_=pos[:])
                    else:
                        nc.scalar.copy(out=paired[:, h, first : first + T_CHUNK], in_=pos[:])

            for n in range(SEQS):
                store_pairs(SMALL_PAIRS, PAIRS, n, h)
            for n in range(SEQS):
                store_pairs(1, SMALL_PAIRS, n, h)
                nc.sync.dma_start(
                    out=out_flat[n * HEADS + h, 0 : PAIR * PADDED - DROPPED].unsqueeze(0),
                    in_=paired[n * PAIRS : n * PAIRS + 1, h, FRONT + DROPPED : PITCH],
                )
